import numpy as np
import ml_dtypes


def mxq(x, axis, fmt="e4m3"):
    dtype, down = {"e4m3": (ml_dtypes.float8_e4m3fn, 7), "e5m2": (ml_dtypes.float8_e5m2, 14)}[fmt]
    v = np.moveaxis(np.asarray(x, np.float32).astype(ml_dtypes.bfloat16).astype(np.float64), axis, -1)
    blocks = v.reshape(v.shape[:-1] + (-1, 32))
    amax = np.abs(blocks).max(-1, keepdims=True)
    byte = np.maximum(np.where(amax > 0, np.frexp(amax)[1] - 1 + 127, 0) - down, 1)
    scale = np.exp2(byte - 127.0)
    codes = (blocks / scale).astype(np.float32).astype(dtype).astype(np.float64)
    return np.moveaxis((codes * scale).reshape(v.shape), -1, axis)


WIDE = False


def mx_kscale(k):
    if not WIDE:
        return np.ones(k)
    levels = np.array([10, -10, 5, -5, 0])
    a = np.random.permutation(np.resize(levels, k // 512 * 4)).reshape(k // 512, 4)
    idx = np.arange(k)
    return np.exp2(a[idx // 512, idx % 128 // 32])


BF16 = ml_dtypes.bfloat16


def bf(x):
    return np.asarray(x, np.float32).astype(BF16)


def f64(x):
    return np.asarray(x).astype(np.float64)


B, F, C, H = 2, 256, 7936, 256
K = C + H


def sigmoid(v):
    return 1.0 / (1.0 + np.exp(-v))


def setup_inputs():
    s = mx_kscale(K)

    def w():
        return bf(np.random.standard_normal((H, K)) / np.sqrt(K) / s[None, :])

    def b():
        return bf(np.random.standard_normal(H) * 0.3)

    return {"x": bf(np.random.standard_normal((B, F, C)) * s[None, None, :C]),
            "hidden_state": bf(np.random.standard_normal((B, H, F)) * s[None, C:, None]),
            "cell_state": bf(np.random.standard_normal((B, H, F))),
            "W_f": w(), "b_f": b(), "W_i": w(), "b_i": b(), "W_o": w(), "b_o": b(), "W_g": w(), "b_g": b()}


def reference(x, hidden_state, cell_state, W_f, b_f, W_i, b_i, W_o, b_o, W_g, b_g):
    xh = np.concatenate([np.swapaxes(f64(x), 1, 2), f64(hidden_state)], axis=1)
    W = np.concatenate([f64(W_f), f64(W_i), f64(W_g), f64(W_o)], axis=0)
    b = np.concatenate([f64(b_f), f64(b_i), f64(b_g), f64(b_o)], axis=0)
    gates = (mxq(W, 1, "e4m3") @ mxq(xh, 1, "e4m3")) + b[None, :, None]
    f_t = sigmoid(gates[:, 0 * H:1 * H])
    i_t = sigmoid(gates[:, 1 * H:2 * H])
    g_t = np.tanh(gates[:, 2 * H:3 * H])
    o_t = sigmoid(gates[:, 3 * H:4 * H])
    new_cell = f64(cell_state) * f_t + i_t * g_t
    new_hidden = np.tanh(new_cell) * o_t
    return (np.swapaxes(new_hidden, 1, 2), new_hidden, new_cell)

@@ -1,0 +1,289 @@
+from contextlib import ExitStack
+
+import concourse.mybir as mybir
+from concourse.masks import make_identity
+
+F32 = mybir.dt.float32
+BF16 = mybir.dt.bfloat16
+U32 = mybir.dt.uint32
+U8 = mybir.dt.uint8
+FP8X4 = mybir.dt.float8_e4m3fn_x4
+ACT = mybir.ActivationFunctionType
+ALU = mybir.AluOpType
+
+P = 128
+PACK = 4
+K_PASS = P * PACK
+PASS_WORDS = K_PASS // 2
+BANK_WORDS = 512
+
+BATCH, FRAMES, CHANNELS, HIDDEN = 2, 256, 7936, 256
+K = CHANNELS + HIDDEN
+PASSES = K // K_PASS
+N = BATCH * FRAMES
+ROW_TILES = N // P
+GATES = 4
+H_TILES = HIDDEN // P
+
+CHUNK_PASSES = 2
+CHUNK_K = CHUNK_PASSES * K_PASS
+CHUNKS = K // CHUNK_K
+LOAD_AHEAD = 3
+
+FLOPS = 2 * GATES * HIDDEN * K * N
+
+
+def tile_batchedlstm_k_kernel(
+    tc, x, hidden_state, cell_state, W_f, b_f, W_i, b_i, W_o, b_o, W_g, b_g, out_0, out_1, out_2
+):
+    nc = tc.nc
+    weights = (W_f, W_i, W_g, W_o)
+    biases = (b_f, b_i, b_g, b_o)
+    gate_functions = (ACT.Sigmoid, ACT.Sigmoid, ACT.Tanh, ACT.Sigmoid)
+    x_rows = x.rearrange("b f c -> (b f) c")
+
+    rounds = [(0, [g]) for g in range(PASSES)]
+    rounds += [(1, [g, g + 1]) for g in range(0, PASSES, 2)]
+
+    with ExitStack() as ctx:
+        ctx.enter_context(tc.manual_schedule())
+        keep = ctx.enter_context(tc.tile_pool(name="keep", bufs=1))
+        x_raw_pool = ctx.enter_context(tc.tile_pool(name="x_raw", bufs=ROW_TILES * (LOAD_AHEAD + 1)))
+        w_raw_pool = ctx.enter_context(tc.tile_pool(name="w_raw", bufs=GATES * (LOAD_AHEAD + 1)))
+        grouped_pool = ctx.enter_context(tc.tile_pool(name="grouped", bufs=4))
+        w_mx_pool = ctx.enter_context(tc.tile_pool(name="w_mx", bufs=4))
+        cell_pool = ctx.enter_context(tc.tile_pool(name="cell", bufs=H_TILES))
+        acc_pool = ctx.enter_context(tc.psum_pool(name="acc", bufs=1))
+        bank_pool = ctx.enter_context(tc.psum_pool(name="bank", bufs=4))
+
+        identity = keep.tile([P, P], F32, name="identity")
+        make_identity(nc, identity[:])
+
+        bias_rows = keep.tile([P, P], BF16, name="bias_rows")
+        nc.vector.memset(bias_rows[:], 0.0)
+        for gate in range(GATES):
+            nc.scalar.dma_start(
+                out=bias_rows[gate * H_TILES : (gate + 1) * H_TILES, :],
+                in_=biases[gate].rearrange("(t p) -> t p", p=P),
+            )
+        bias_columns = keep.tile([P, GATES * H_TILES], F32, name="bias_columns")
+
+        warm = keep.tile([P, 1], F32, name="warm")
+        nc.vector.memset(warm[:], 0.0)
+        nc.scalar.activation(out=warm[:], in_=warm[:], func=ACT.Sigmoid)
+
+        def spread_biases():
+            bias_rows_f32 = keep.tile([P, P], F32, name="bias_rows_f32")
+            nc.vector.tensor_copy(out=bias_rows_f32[:], in_=bias_rows[:])
+            bank = bank_pool.tile([P, BANK_WORDS], F32, name="bank")
+            nc.tensor.transpose(bank[:, :P], bias_rows_f32[:], identity[:])
+            nc.vector.tensor_copy(out=bias_columns[:], in_=bank[:, : GATES * H_TILES])
+
+        x_raw = {}
+        w_raw = {}
+        cell_raw = {}
+        hidden_raw = keep.tile([P, BATCH, 2 * FRAMES], BF16, name="hidden_raw")
+
+        def load_chunk(step):
+            h_tile, chunk = divmod(step, CHUNKS)
+            h_rows = slice(h_tile * P, (h_tile + 1) * P)
+            k0 = chunk * CHUNK_K
+            if h_tile == 0:
+                width = min(CHUNK_K, CHANNELS - k0)
+                for r in range(ROW_TILES):
+                    raw = x_raw_pool.tile([P, CHUNK_K], BF16, name="x_raw")
+                    nc.sync.dma_start(
+                        out=raw[:, :width], in_=x_rows[r * P : (r + 1) * P, k0 : k0 + width]
+                    )
+                    x_raw[(chunk, r)] = raw
+                if width < CHUNK_K:
+                    nc.sync.dma_start(
+                        out=hidden_raw[:],
+                        in_=hidden_state.rearrange("b (p e) f -> p b (e f)", e=2),
+                    )
+            for gate in range(GATES):
+                raw = w_raw_pool.tile([P, CHUNK_K], BF16, name="w_raw")
+                nc.sync.dma_start(out=raw[:], in_=weights[gate][h_rows, k0 : k0 + CHUNK_K])
+                w_raw[(h_tile, chunk, gate)] = raw
+            if chunk == CHUNKS - 1:
+                raw = cell_pool.tile([P, BATCH, FRAMES], BF16, name="cell_raw")
+                nc.sync.dma_start(out=raw[:], in_=cell_state.rearrange("b h f -> h b f")[h_rows])
+                cell_raw[h_tile] = raw
+
+        def transpose_operand(sources, first_word, first_copy):
+            grouped = grouped_pool.tile([P, GATES * P * PACK], BF16, align_bytes=64, name="grouped")
+            grouped_words = grouped[:].bitcast(F32).rearrange("p (s n u) -> p s n u", s=4, u=2)
+            for pair in range(2):
+                bank = bank_pool.tile([P, BANK_WORDS], F32, name="bank")
+                planes = bank[:].rearrange("p (s u n) -> p s u n", s=2, u=2)
+                for s in range(2):
+                    words = sources[2 * pair + s][:].bitcast(F32)
+                    for u in range(2):
+                        w0 = first_word + u * P
+                        nc.tensor.transpose(planes[:, s, u, :], words[:, w0 : w0 + P], identity[:])
+                copy_out = first_copy if pair == 0 else nc.scalar.copy
+                copy_out(
+                    out=grouped_words[:, 2 * pair : 2 * pair + 2],
+                    in_=planes.rearrange("p s u n -> p s n u"),
+                )
+            return grouped
+
+        def transpose_last_xh(sources, first_word):
+            grouped = grouped_pool.tile([P, N * PACK], BF16, align_bytes=64, name="grouped")
+            values = grouped[:].rearrange("p (b f t) -> p b f t", b=BATCH, t=PACK)
+            nc.vector.tensor_copy(
+                out=values[:, :, :, 2:4],
+                in_=hidden_raw[:].rearrange("p b (e f) -> p b f e", e=2),
+            )
+            bank = bank_pool.tile([P, BANK_WORDS], F32, name="bank")
+            for r in range(ROW_TILES):
+                words = sources[r][:].bitcast(F32)
+                nc.tensor.transpose(
+                    bank[:, r * P : (r + 1) * P], words[:, first_word : first_word + P], identity[:]
+                )
+            grouped_words = grouped[:].bitcast(F32).rearrange("p (n u) -> p n u", u=2)
+            nc.vector.tensor_copy(out=grouped_words[:, :, 0], in_=bank[:])
+            return grouped
+
+        x_codes = {}
+        x_scales = {}
+        w_codes = {}
+        w_scales = {}
+        staged = {}
+
+        def stage(index):
+            h_tile, passes = rounds[index]
+            chunk, pass_in_chunk = divmod(passes[0], CHUNK_PASSES)
+            step = h_tile * CHUNKS + chunk
+            if pass_in_chunk == 0 and step + LOAD_AHEAD < H_TILES * CHUNKS:
+                load_chunk(step + LOAD_AHEAD)
+            staged[index] = []
+            first_copy = nc.vector.tensor_copy
+            for g in passes:
+                first_word = (g % CHUNK_PASSES) * PASS_WORDS
+                if h_tile == 0:
+                    sources = [x_raw[(chunk, r)] for r in range(ROW_TILES)]
+                    if g < PASSES - 1:
+                        grouped = transpose_operand(sources, first_word, first_copy)
+                    else:
+                        grouped = transpose_last_xh(sources, first_word)
+                    first_copy = nc.scalar.copy
+                    x_codes[g] = keep.tile([P, N], U32, align_bytes=64, name="x_codes%d" % g)
+                    x_scales[g] = keep.tile([P, N], U8, align_bytes=64, name="x_scales%d" % g)
+                    staged[index].append((grouped, x_codes[g], x_scales[g]))
+                sources = [w_raw[(h_tile, chunk, gate)] for gate in range(GATES)]
+                grouped = transpose_operand(sources, first_word, first_copy)
+                first_copy = nc.scalar.copy
+                codes = w_mx_pool.tile([P, GATES * P], U32, align_bytes=64, name="w_codes")
+                scales = w_mx_pool.tile([P, GATES * P], U8, align_bytes=64, name="w_scales")
+                w_codes[(h_tile, g)] = codes
+                w_scales[(h_tile, g)] = scales
+                staged[index].append((grouped, codes, scales))
+
+        def quantise(index):
+            for grouped, codes, scales in staged[index]:
+                nc.vector.quantize_mx(out=codes[:].bitcast(FP8X4), scales=scales[:], in_=grouped[:])
+
+        acc = {}
+
+        def multiply(index):
+            h_tile, passes = rounds[index]
+            for gate in range(GATES):
+                if passes[0] == 0:
+                    acc[(h_tile, gate)] = acc_pool.tile([P, N], F32, name="acc%d" % gate)
+                gate_columns = slice(gate * P, (gate + 1) * P)
+                for g in passes:
+                    nc.tensor.matmul_mx(
+                        out=acc[(h_tile, gate)][:],
+                        lhsT=w_codes[(h_tile, g)][:, gate_columns].bitcast(FP8X4),
+                        lhsT_scale=w_scales[(h_tile, g)][:, gate_columns],
+                        rhs=x_codes[g][:].bitcast(FP8X4),
+                        rhs_scale=x_scales[g][:],
+                        start=(g == 0),
+                        stop=(g == PASSES - 1),
+                    )
+
+        let_out = {}
+        new_cell = {}
+        new_hidden = {}
+
+        def h_tile_closed_by(index):
+            if 0 <= index < len(rounds) and rounds[index][1][-1] == PASSES - 1:
+                return rounds[index][0]
+            return None
+
+        def update_cell(h_tile):
+            h_rows = slice(h_tile * P, (h_tile + 1) * P)
+            activated = []
+            for gate in range(GATES):
+                gate_tile = cell_pool.tile([P, N], F32, name="gate%d" % gate)
+                bias_column = gate * H_TILES + h_tile
+                nc.scalar.activation(
+                    out=gate_tile[:],
+                    in_=acc[(h_tile, gate)][:],
+                    func=gate_functions[gate],
+                    bias=bias_columns[:, bias_column : bias_column + 1],
+                    scale=1.0,
+                )
+                activated.append(gate_tile)
+            forget, take_in, candidate, let_out[h_tile] = activated
+            kept = cell_pool.tile([P, N], F32, name="kept")
+            nc.vector.tensor_tensor(
+                out=kept[:],
+                in0=forget[:],
+                in1=cell_raw[h_tile][:].rearrange("p b f -> p (b f)"),
+                op=ALU.mult,
+            )
+            added = cell_pool.tile([P, N], F32, name="added")
+            nc.vector.tensor_tensor(out=added[:], in0=take_in[:], in1=candidate[:], op=ALU.mult)
+            new_cell[h_tile] = cell_pool.tile([P, N], F32, name="new_cell")
+            nc.vector.tensor_tensor(out=new_cell[h_tile][:], in0=kept[:], in1=added[:], op=ALU.add)
+            nc.sync.dma_start(
+                out=out_2.rearrange("b h f -> h b f")[h_rows],
+                in_=new_cell[h_tile][:].rearrange("p (b f) -> p b f", b=BATCH),
+            )
+
+        def update_hidden(h_tile):
+            h_rows = slice(h_tile * P, (h_tile + 1) * P)
+            squashed = cell_pool.tile([P, N], F32, name="squashed")
+            nc.scalar.activation(out=squashed[:], in_=new_cell[h_tile][:], func=ACT.Tanh)
+            new_hidden[h_tile] = cell_pool.tile([P, N], F32, name="new_hidden")
+            nc.vector.tensor_tensor(
+                out=new_hidden[h_tile][:], in0=squashed[:], in1=let_out[h_tile][:], op=ALU.mult
+            )
+            nc.sync.dma_start(
+                out=out_1.rearrange("b h f -> h b f")[h_rows],
+                in_=new_hidden[h_tile][:].rearrange("p (b f) -> p b f", b=BATCH),
+            )
+
+        def store_hidden_transposed(h_tile):
+            bank = bank_pool.tile([P, BANK_WORDS], F32, name="bank")
+            for r in range(ROW_TILES):
+                tile_columns = slice(r * P, (r + 1) * P)
+                nc.tensor.transpose(
+                    bank[:, tile_columns], new_hidden[h_tile][:, tile_columns], identity[:]
+                )
+            flipped = cell_pool.tile([P, N], F32, name="flipped")
+            nc.vector.tensor_copy(out=flipped[:], in_=bank[:])
+            nc.sync.dma_start(
+                out=out_0.rearrange("b (t p) h -> p (b t) h", p=P)[:, :, h_tile * P : (h_tile + 1) * P],
+                in_=flipped[:].rearrange("p (r h) -> p r h", r=ROW_TILES),
+            )
+
+        for step in range(LOAD_AHEAD):
+            load_chunk(step)
+        for index in range(len(rounds) + 3):
+            if h_tile_closed_by(index - 3) is not None:
+                store_hidden_transposed(h_tile_closed_by(index - 3))
+            if index < len(rounds):
+                stage(index)
+            if index == 0:
+                spread_biases()
+            if 0 <= index - 1 < len(rounds):
+                multiply(index - 1)
+            if index < len(rounds):
+                quantise(index)
+            if h_tile_closed_by(index - 1) is not None:
+                update_cell(h_tile_closed_by(index - 1))
+            if h_tile_closed_by(index - 2) is not None:
+                update_hidden(h_tile_closed_by(index - 2))

@@ -30,6 +30,10 @@ CHUNK_K = CHUNK_PASSES * K_PASS
 CHUNKS = K // CHUNK_K
 LOAD_AHEAD = 3
 
+FREE_BANKS = 4
+OPERAND_BANKS = 2
+ROUND_BANKS = 2 * FREE_BANKS
+
 FLOPS = 2 * GATES * HIDDEN * K * N
 
 
@@ -42,19 +46,21 @@ def tile_batchedlstm_k_kernel(
     gate_functions = (ACT.Sigmoid, ACT.Sigmoid, ACT.Tanh, ACT.Sigmoid)
     x_rows = x.rearrange("b f c -> (b f) c")
 
-    rounds = [(0, [g]) for g in range(PASSES)]
-    rounds += [(1, [g, g + 1]) for g in range(0, PASSES, 2)]
+    rounds = []
+    for h_tile, operands_a_pass in ((0, 2), (1, 1)):
+        round_passes = ROUND_BANKS // (OPERAND_BANKS * operands_a_pass)
+        rounds += [(h_tile, list(range(g, g + round_passes))) for g in range(0, PASSES, round_passes)]
 
     with ExitStack() as ctx:
         ctx.enter_context(tc.manual_schedule())
         keep = ctx.enter_context(tc.tile_pool(name="keep", bufs=1))
         x_raw_pool = ctx.enter_context(tc.tile_pool(name="x_raw", bufs=ROW_TILES * (LOAD_AHEAD + 1)))
         w_raw_pool = ctx.enter_context(tc.tile_pool(name="w_raw", bufs=GATES * (LOAD_AHEAD + 1)))
-        grouped_pool = ctx.enter_context(tc.tile_pool(name="grouped", bufs=4))
-        w_mx_pool = ctx.enter_context(tc.tile_pool(name="w_mx", bufs=4))
+        grouped_pool = ctx.enter_context(tc.tile_pool(name="grouped", bufs=8))
+        w_mx_pool = ctx.enter_context(tc.tile_pool(name="w_mx", bufs=8))
         cell_pool = ctx.enter_context(tc.tile_pool(name="cell", bufs=H_TILES))
         acc_pool = ctx.enter_context(tc.psum_pool(name="acc", bufs=1))
-        bank_pool = ctx.enter_context(tc.psum_pool(name="bank", bufs=4))
+        bank_pool = ctx.enter_context(tc.psum_pool(name="bank", bufs=FREE_BANKS))
 
         identity = keep.tile([P, P], F32, name="identity")
         make_identity(nc, identity[:])
@@ -68,21 +74,30 @@ def tile_batchedlstm_k_kernel(
             )
         bias_columns = keep.tile([P, GATES * H_TILES], F32, name="bias_columns")
 
+        hidden_raw = keep.tile([P, BATCH, 2 * FRAMES], BF16, name="hidden_raw")
+        nc.scalar.dma_start(
+            out=hidden_raw[:], in_=hidden_state.rearrange("b (p e) f -> p b (e f)", e=2)
+        )
+        last_xh = keep.tile([P, N * PACK], BF16, align_bytes=64, name="last_xh")
+
         warm = keep.tile([P, 1], F32, name="warm")
         nc.vector.memset(warm[:], 0.0)
         nc.scalar.activation(out=warm[:], in_=warm[:], func=ACT.Sigmoid)
 
-        def spread_biases():
+        def prepare_small_inputs():
             bias_rows_f32 = keep.tile([P, P], F32, name="bias_rows_f32")
             nc.vector.tensor_copy(out=bias_rows_f32[:], in_=bias_rows[:])
             bank = bank_pool.tile([P, BANK_WORDS], F32, name="bank")
             nc.tensor.transpose(bank[:, :P], bias_rows_f32[:], identity[:])
             nc.vector.tensor_copy(out=bias_columns[:], in_=bank[:, : GATES * H_TILES])
+            nc.vector.tensor_copy(
+                out=last_xh[:].rearrange("p (b f t) -> p b f t", b=BATCH, t=PACK)[:, :, :, 2:4],
+                in_=hidden_raw[:].rearrange("p b (e f) -> p b f e", e=2),
+            )
 
         x_raw = {}
         w_raw = {}
         cell_raw = {}
-        hidden_raw = keep.tile([P, BATCH, 2 * FRAMES], BF16, name="hidden_raw")
 
         def load_chunk(step):
             h_tile, chunk = divmod(step, CHUNKS)
@@ -96,11 +111,6 @@ def tile_batchedlstm_k_kernel(
                         out=raw[:, :width], in_=x_rows[r * P : (r + 1) * P, k0 : k0 + width]
                     )
                     x_raw[(chunk, r)] = raw
-                if width < CHUNK_K:
-                    nc.sync.dma_start(
-                        out=hidden_raw[:],
-                        in_=hidden_state.rearrange("b (p e) f -> p b (e f)", e=2),
-                    )
             for gate in range(GATES):
                 raw = w_raw_pool.tile([P, CHUNK_K], BF16, name="w_raw")
                 nc.sync.dma_start(out=raw[:], in_=weights[gate][h_rows, k0 : k0 + CHUNK_K])
@@ -111,9 +121,9 @@ def tile_batchedlstm_k_kernel(
                 cell_raw[h_tile] = raw
 
         def transpose_operand(sources, first_word, first_copy):
-            grouped = grouped_pool.tile([P, GATES * P * PACK], BF16, align_bytes=64, name="grouped")
+            grouped = grouped_pool.tile([P, N * PACK], BF16, align_bytes=64, name="grouped")
             grouped_words = grouped[:].bitcast(F32).rearrange("p (s n u) -> p s n u", s=4, u=2)
-            for pair in range(2):
+            for pair in range(OPERAND_BANKS):
                 bank = bank_pool.tile([P, BANK_WORDS], F32, name="bank")
                 planes = bank[:].rearrange("p (s u n) -> p s u n", s=2, u=2)
                 for s in range(2):
@@ -129,21 +139,15 @@ def tile_batchedlstm_k_kernel(
             return grouped
 
         def transpose_last_xh(sources, first_word):
-            grouped = grouped_pool.tile([P, N * PACK], BF16, align_bytes=64, name="grouped")
-            values = grouped[:].rearrange("p (b f t) -> p b f t", b=BATCH, t=PACK)
-            nc.vector.tensor_copy(
-                out=values[:, :, :, 2:4],
-                in_=hidden_raw[:].rearrange("p b (e f) -> p b f e", e=2),
-            )
             bank = bank_pool.tile([P, BANK_WORDS], F32, name="bank")
             for r in range(ROW_TILES):
                 words = sources[r][:].bitcast(F32)
                 nc.tensor.transpose(
                     bank[:, r * P : (r + 1) * P], words[:, first_word : first_word + P], identity[:]
                 )
-            grouped_words = grouped[:].bitcast(F32).rearrange("p (n u) -> p n u", u=2)
-            nc.vector.tensor_copy(out=grouped_words[:, :, 0], in_=bank[:])
-            return grouped
+            last_xh_words = last_xh[:].bitcast(F32).rearrange("p (n u) -> p n u", u=2)
+            nc.vector.tensor_copy(out=last_xh_words[:, :, 0], in_=bank[:])
+            return last_xh
 
         x_codes = {}
         x_scales = {}
@@ -153,27 +157,30 @@ def tile_batchedlstm_k_kernel(
 
         def stage(index):
             h_tile, passes = rounds[index]
-            chunk, pass_in_chunk = divmod(passes[0], CHUNK_PASSES)
-            step = h_tile * CHUNKS + chunk
-            if pass_in_chunk == 0 and step + LOAD_AHEAD < H_TILES * CHUNKS:
-                load_chunk(step + LOAD_AHEAD)
             staged[index] = []
-            first_copy = nc.vector.tensor_copy
-            for g in passes:
-                first_word = (g % CHUNK_PASSES) * PASS_WORDS
-                if h_tile == 0:
-                    sources = [x_raw[(chunk, r)] for r in range(ROW_TILES)]
+
+            def copy_for_first_bank():
+                early = len(staged[index]) * OPERAND_BANKS < FREE_BANKS
+                return nc.vector.tensor_copy if early else nc.scalar.copy
+
+            if h_tile == 0:
+                for g in passes:
+                    sources = [x_raw[(g // CHUNK_PASSES, r)] for r in range(ROW_TILES)]
+                    first_word = (g % CHUNK_PASSES) * PASS_WORDS
                     if g < PASSES - 1:
-                        grouped = transpose_operand(sources, first_word, first_copy)
+                        grouped = transpose_operand(sources, first_word, copy_for_first_bank())
                     else:
                         grouped = transpose_last_xh(sources, first_word)
-                    first_copy = nc.scalar.copy
                     x_codes[g] = keep.tile([P, N], U32, align_bytes=64, name="x_codes%d" % g)
                     x_scales[g] = keep.tile([P, N], U8, align_bytes=64, name="x_scales%d" % g)
                     staged[index].append((grouped, x_codes[g], x_scales[g]))
+            for g in passes:
+                chunk, pass_in_chunk = divmod(g, CHUNK_PASSES)
+                step = h_tile * CHUNKS + chunk
+                if pass_in_chunk == 0 and step + LOAD_AHEAD < H_TILES * CHUNKS:
+                    load_chunk(step + LOAD_AHEAD)
                 sources = [w_raw[(h_tile, chunk, gate)] for gate in range(GATES)]
-                grouped = transpose_operand(sources, first_word, first_copy)
-                first_copy = nc.scalar.copy
+                grouped = transpose_operand(sources, pass_in_chunk * PASS_WORDS, copy_for_first_bank())
                 codes = w_mx_pool.tile([P, GATES * P], U32, align_bytes=64, name="w_codes")
                 scales = w_mx_pool.tile([P, GATES * P], U8, align_bytes=64, name="w_scales")
                 w_codes[(h_tile, g)] = codes
@@ -203,30 +210,24 @@ def tile_batchedlstm_k_kernel(
                         stop=(g == PASSES - 1),
                     )
 
-        let_out = {}
+        activated = {}
         new_cell = {}
         new_hidden = {}
 
-        def h_tile_closed_by(index):
-            if 0 <= index < len(rounds) and rounds[index][1][-1] == PASSES - 1:
-                return rounds[index][0]
-            return None
-
-        def update_cell(h_tile):
-            h_rows = slice(h_tile * P, (h_tile + 1) * P)
-            activated = []
+        def activate_gates(h_tile):
             for gate in range(GATES):
-                gate_tile = cell_pool.tile([P, N], F32, name="gate%d" % gate)
+                activated[(h_tile, gate)] = cell_pool.tile([P, N], F32, name="gate%d" % gate)
                 bias_column = gate * H_TILES + h_tile
                 nc.scalar.activation(
-                    out=gate_tile[:],
+                    out=activated[(h_tile, gate)][:],
                     in_=acc[(h_tile, gate)][:],
                     func=gate_functions[gate],
                     bias=bias_columns[:, bias_column : bias_column + 1],
                     scale=1.0,
                 )
-                activated.append(gate_tile)
-            forget, take_in, candidate, let_out[h_tile] = activated
+
+        def update_cell(h_tile):
+            forget, take_in, candidate = [activated[(h_tile, gate)] for gate in range(3)]
             kept = cell_pool.tile([P, N], F32, name="kept")
             nc.vector.tensor_tensor(
                 out=kept[:],
@@ -239,20 +240,19 @@ def tile_batchedlstm_k_kernel(
             new_cell[h_tile] = cell_pool.tile([P, N], F32, name="new_cell")
             nc.vector.tensor_tensor(out=new_cell[h_tile][:], in0=kept[:], in1=added[:], op=ALU.add)
             nc.sync.dma_start(
-                out=out_2.rearrange("b h f -> h b f")[h_rows],
+                out=out_2.rearrange("b h f -> h b f")[h_tile * P : (h_tile + 1) * P],
                 in_=new_cell[h_tile][:].rearrange("p (b f) -> p b f", b=BATCH),
             )
 
         def update_hidden(h_tile):
-            h_rows = slice(h_tile * P, (h_tile + 1) * P)
             squashed = cell_pool.tile([P, N], F32, name="squashed")
             nc.scalar.activation(out=squashed[:], in_=new_cell[h_tile][:], func=ACT.Tanh)
             new_hidden[h_tile] = cell_pool.tile([P, N], F32, name="new_hidden")
             nc.vector.tensor_tensor(
-                out=new_hidden[h_tile][:], in0=squashed[:], in1=let_out[h_tile][:], op=ALU.mult
+                out=new_hidden[h_tile][:], in0=squashed[:], in1=activated[(h_tile, 3)][:], op=ALU.mult
             )
             nc.sync.dma_start(
-                out=out_1.rearrange("b h f -> h b f")[h_rows],
+                out=out_1.rearrange("b h f -> h b f")[h_tile * P : (h_tile + 1) * P],
                 in_=new_hidden[h_tile][:].rearrange("p (b f) -> p b f", b=BATCH),
             )
 
@@ -270,6 +270,11 @@ def tile_batchedlstm_k_kernel(
                 in_=flipped[:].rearrange("p (r h) -> p r h", r=ROW_TILES),
             )
 
+        def h_tile_closed_by(index):
+            if 0 <= index < len(rounds) and rounds[index][1][-1] == PASSES - 1:
+                return rounds[index][0]
+            return None
+
         for step in range(LOAD_AHEAD):
             load_chunk(step)
         for index in range(len(rounds) + 3):
@@ -278,12 +283,14 @@ def tile_batchedlstm_k_kernel(
             if index < len(rounds):
                 stage(index)
             if index == 0:
-                spread_biases()
+                prepare_small_inputs()
             if 0 <= index - 1 < len(rounds):
                 multiply(index - 1)
+            if h_tile_closed_by(index - 2) is not None:
+                update_cell(h_tile_closed_by(index - 2))
             if index < len(rounds):
                 quantise(index)
             if h_tile_closed_by(index - 1) is not None:
-                update_cell(h_tile_closed_by(index - 1))
+                activate_gates(h_tile_closed_by(index - 1))
             if h_tile_closed_by(index - 2) is not None:
                 update_hidden(h_tile_closed_by(index - 2))

@@ -32,7 +32,11 @@ LOAD_AHEAD = 3
 
 FREE_BANKS = 4
 OPERAND_BANKS = 2
-ROUND_BANKS = 2 * FREE_BANKS
+BANK_TILES = 2
+BANK_COLUMNS = BANK_TILES * P
+
+IDLE_MATMULS = 3
+FLIP_LAG = 5
 
 FLOPS = 2 * GATES * HIDDEN * K * N
 
@@ -48,7 +52,7 @@ def tile_batchedlstm_k_kernel(
 
     rounds = []
     for h_tile, operands_a_pass in ((0, 2), (1, 1)):
-        round_passes = ROUND_BANKS // (OPERAND_BANKS * operands_a_pass)
+        round_passes = FREE_BANKS // (OPERAND_BANKS * operands_a_pass)
         rounds += [(h_tile, list(range(g, g + round_passes))) for g in range(0, PASSES, round_passes)]
 
     with ExitStack() as ctx:
@@ -56,14 +60,16 @@ def tile_batchedlstm_k_kernel(
         keep = ctx.enter_context(tc.tile_pool(name="keep", bufs=1))
         x_raw_pool = ctx.enter_context(tc.tile_pool(name="x_raw", bufs=ROW_TILES * (LOAD_AHEAD + 1)))
         w_raw_pool = ctx.enter_context(tc.tile_pool(name="w_raw", bufs=GATES * (LOAD_AHEAD + 1)))
-        grouped_pool = ctx.enter_context(tc.tile_pool(name="grouped", bufs=8))
-        w_mx_pool = ctx.enter_context(tc.tile_pool(name="w_mx", bufs=8))
-        cell_pool = ctx.enter_context(tc.tile_pool(name="cell", bufs=H_TILES))
+        grouped_pool = ctx.enter_context(tc.tile_pool(name="grouped", bufs=2 * FREE_BANKS))
+        w_mx_pool = ctx.enter_context(tc.tile_pool(name="w_mx", bufs=4))
+        cell_pool = ctx.enter_context(tc.tile_pool(name="cell", bufs=H_TILES * BATCH))
         acc_pool = ctx.enter_context(tc.psum_pool(name="acc", bufs=1))
         bank_pool = ctx.enter_context(tc.psum_pool(name="bank", bufs=FREE_BANKS))
 
         identity = keep.tile([P, P], F32, name="identity")
         make_identity(nc, identity[:])
+        zeros = keep.tile([P, N], BF16, name="zeros")
+        nc.vector.memset(zeros[:], 0.0)
 
         bias_rows = keep.tile([P, P], BF16, name="bias_rows")
         nc.vector.memset(bias_rows[:], 0.0)
@@ -95,6 +101,12 @@ def tile_batchedlstm_k_kernel(
                 in_=hidden_raw[:].rearrange("p b (e f) -> p b f e", e=2),
             )
 
+        idle_bank = acc_pool.tile([P, N], F32, name="acc0")
+
+        def hold_clock():
+            for repeat in range(IDLE_MATMULS):
+                nc.tensor.matmul(idle_bank[:], lhsT=zeros[:, :P], rhs=zeros[:], start=True, stop=True)
+
         x_raw = {}
         w_raw = {}
         cell_raw = {}
@@ -120,25 +132,29 @@ def tile_batchedlstm_k_kernel(
                 nc.sync.dma_start(out=raw[:], in_=cell_state.rearrange("b h f -> h b f")[h_rows])
                 cell_raw[h_tile] = raw
 
-        def transpose_operand(sources, first_word, first_copy):
-            grouped = grouped_pool.tile([P, N * PACK], BF16, align_bytes=64, name="grouped")
-            grouped_words = grouped[:].bitcast(F32).rearrange("p (s n u) -> p s n u", s=4, u=2)
-            for pair in range(OPERAND_BANKS):
+        staged = {}
+
+        def transpose_operand(index, sources, first_word, codes, scales, vector_helps):
+            for half in range(OPERAND_BANKS):
                 bank = bank_pool.tile([P, BANK_WORDS], F32, name="bank")
-                planes = bank[:].rearrange("p (s u n) -> p s u n", s=2, u=2)
-                for s in range(2):
-                    words = sources[2 * pair + s][:].bitcast(F32)
+                planes = bank[:].rearrange("p (s u n) -> p s u n", s=BANK_TILES, u=2)
+                for s in range(BANK_TILES):
+                    words = sources[BANK_TILES * half + s][:].bitcast(F32)
                     for u in range(2):
                         w0 = first_word + u * P
                         nc.tensor.transpose(planes[:, s, u, :], words[:, w0 : w0 + P], identity[:])
-                copy_out = first_copy if pair == 0 else nc.scalar.copy
+                grouped = grouped_pool.tile(
+                    [P, BANK_COLUMNS * PACK], BF16, align_bytes=64, name="grouped"
+                )
+                copy_out = nc.vector.tensor_copy if vector_helps and half == 1 else nc.scalar.copy
                 copy_out(
-                    out=grouped_words[:, 2 * pair : 2 * pair + 2],
+                    out=grouped[:].bitcast(F32).rearrange("p (s n u) -> p s n u", s=BANK_TILES, u=2),
                     in_=planes.rearrange("p s u n -> p s n u"),
                 )
-            return grouped
+                columns = slice(half * BANK_COLUMNS, (half + 1) * BANK_COLUMNS)
+                staged[index].append((grouped[:], codes[:, columns], scales[:, columns]))
 
-        def transpose_last_xh(sources, first_word):
+        def transpose_last_xh(index, sources, first_word, codes, scales):
             bank = bank_pool.tile([P, BANK_WORDS], F32, name="bank")
             for r in range(ROW_TILES):
                 words = sources[r][:].bitcast(F32)
@@ -147,49 +163,45 @@ def tile_batchedlstm_k_kernel(
                 )
             last_xh_words = last_xh[:].bitcast(F32).rearrange("p (n u) -> p n u", u=2)
             nc.vector.tensor_copy(out=last_xh_words[:, :, 0], in_=bank[:])
-            return last_xh
+            staged[index].append((last_xh[:], codes[:], scales[:]))
 
         x_codes = {}
         x_scales = {}
         w_codes = {}
         w_scales = {}
-        staged = {}
 
         def stage(index):
             h_tile, passes = rounds[index]
             staged[index] = []
-
-            def copy_for_first_bank():
-                early = len(staged[index]) * OPERAND_BANKS < FREE_BANKS
-                return nc.vector.tensor_copy if early else nc.scalar.copy
-
-            if h_tile == 0:
-                for g in passes:
-                    sources = [x_raw[(g // CHUNK_PASSES, r)] for r in range(ROW_TILES)]
-                    first_word = (g % CHUNK_PASSES) * PASS_WORDS
-                    if g < PASSES - 1:
-                        grouped = transpose_operand(sources, first_word, copy_for_first_bank())
-                    else:
-                        grouped = transpose_last_xh(sources, first_word)
-                    x_codes[g] = keep.tile([P, N], U32, align_bytes=64, name="x_codes%d" % g)
-                    x_scales[g] = keep.tile([P, N], U8, align_bytes=64, name="x_scales%d" % g)
-                    staged[index].append((grouped, x_codes[g], x_scales[g]))
             for g in passes:
                 chunk, pass_in_chunk = divmod(g, CHUNK_PASSES)
+                first_word = pass_in_chunk * PASS_WORDS
+                if h_tile == 0:
+                    sources = [x_raw[(chunk, r)] for r in range(ROW_TILES)]
+                    x_codes[g] = keep.tile([P, N], U32, align_bytes=64, name="x_codes%d" % g)
+                    x_scales[g] = keep.tile([P, N], U8, align_bytes=64, name="x_scales%d" % g)
+                    if g < PASSES - 1:
+                        transpose_operand(index, sources, first_word, x_codes[g], x_scales[g], True)
+                    else:
+                        transpose_last_xh(index, sources, first_word, x_codes[g], x_scales[g])
+                    if index == 0:
+                        hold_clock()
                 step = h_tile * CHUNKS + chunk
                 if pass_in_chunk == 0 and step + LOAD_AHEAD < H_TILES * CHUNKS:
                     load_chunk(step + LOAD_AHEAD)
                 sources = [w_raw[(h_tile, chunk, gate)] for gate in range(GATES)]
-                grouped = transpose_operand(sources, pass_in_chunk * PASS_WORDS, copy_for_first_bank())
                 codes = w_mx_pool.tile([P, GATES * P], U32, align_bytes=64, name="w_codes")
                 scales = w_mx_pool.tile([P, GATES * P], U8, align_bytes=64, name="w_scales")
                 w_codes[(h_tile, g)] = codes
                 w_scales[(h_tile, g)] = scales
-                staged[index].append((grouped, codes, scales))
+                first_operand = len(staged[index]) == 0
+                transpose_operand(index, sources, first_word, codes, scales, first_operand)
+                if index == 0:
+                    hold_clock()
 
         def quantise(index):
             for grouped, codes, scales in staged[index]:
-                nc.vector.quantize_mx(out=codes[:].bitcast(FP8X4), scales=scales[:], in_=grouped[:])
+                nc.vector.quantize_mx(out=codes.bitcast(FP8X4), scales=scales, in_=grouped)
 
         acc = {}
 
@@ -214,61 +226,77 @@ def tile_batchedlstm_k_kernel(
         new_cell = {}
         new_hidden = {}
 
+        def cell_tile(name):
+            return cell_pool.tile([P, FRAMES], F32, name=name)
+
         def activate_gates(h_tile):
             for gate in range(GATES):
-                activated[(h_tile, gate)] = cell_pool.tile([P, N], F32, name="gate%d" % gate)
                 bias_column = gate * H_TILES + h_tile
-                nc.scalar.activation(
-                    out=activated[(h_tile, gate)][:],
-                    in_=acc[(h_tile, gate)][:],
-                    func=gate_functions[gate],
-                    bias=bias_columns[:, bias_column : bias_column + 1],
-                    scale=1.0,
-                )
+                for b in range(BATCH):
+                    activated[(h_tile, gate, b)] = cell_tile("gate%d" % gate)
+                    nc.scalar.activation(
+                        out=activated[(h_tile, gate, b)][:],
+                        in_=acc[(h_tile, gate)][:, b * FRAMES : (b + 1) * FRAMES],
+                        func=gate_functions[gate],
+                        bias=bias_columns[:, bias_column : bias_column + 1],
+                        scale=1.0,
+                    )
 
         def update_cell(h_tile):
-            forget, take_in, candidate = [activated[(h_tile, gate)] for gate in range(3)]
-            kept = cell_pool.tile([P, N], F32, name="kept")
-            nc.vector.tensor_tensor(
-                out=kept[:],
-                in0=forget[:],
-                in1=cell_raw[h_tile][:].rearrange("p b f -> p (b f)"),
-                op=ALU.mult,
-            )
-            added = cell_pool.tile([P, N], F32, name="added")
-            nc.vector.tensor_tensor(out=added[:], in0=take_in[:], in1=candidate[:], op=ALU.mult)
-            new_cell[h_tile] = cell_pool.tile([P, N], F32, name="new_cell")
-            nc.vector.tensor_tensor(out=new_cell[h_tile][:], in0=kept[:], in1=added[:], op=ALU.add)
-            nc.sync.dma_start(
-                out=out_2.rearrange("b h f -> h b f")[h_tile * P : (h_tile + 1) * P],
-                in_=new_cell[h_tile][:].rearrange("p (b f) -> p b f", b=BATCH),
-            )
+            h_rows = slice(h_tile * P, (h_tile + 1) * P)
+            kept = {}
+            for b in range(BATCH):
+                kept[b] = cell_tile("kept")
+                nc.vector.tensor_tensor(
+                    out=kept[b][:],
+                    in0=activated[(h_tile, 0, b)][:],
+                    in1=cell_raw[h_tile][:, b, :],
+                    op=ALU.mult,
+                )
+            for b in range(BATCH):
+                added = cell_tile("added")
+                nc.vector.tensor_tensor(
+                    out=added[:],
+                    in0=activated[(h_tile, 1, b)][:],
+                    in1=activated[(h_tile, 2, b)][:],
+                    op=ALU.mult,
+                )
+                new_cell[(h_tile, b)] = cell_tile("new_cell")
+                nc.vector.tensor_tensor(
+                    out=new_cell[(h_tile, b)][:], in0=kept[b][:], in1=added[:], op=ALU.add
+                )
+                nc.sync.dma_start(out=out_2[b, h_rows, :], in_=new_cell[(h_tile, b)][:])
 
         def update_hidden(h_tile):
-            squashed = cell_pool.tile([P, N], F32, name="squashed")
-            nc.scalar.activation(out=squashed[:], in_=new_cell[h_tile][:], func=ACT.Tanh)
-            new_hidden[h_tile] = cell_pool.tile([P, N], F32, name="new_hidden")
-            nc.vector.tensor_tensor(
-                out=new_hidden[h_tile][:], in0=squashed[:], in1=activated[(h_tile, 3)][:], op=ALU.mult
-            )
-            nc.sync.dma_start(
-                out=out_1.rearrange("b h f -> h b f")[h_tile * P : (h_tile + 1) * P],
-                in_=new_hidden[h_tile][:].rearrange("p (b f) -> p b f", b=BATCH),
-            )
+            h_rows = slice(h_tile * P, (h_tile + 1) * P)
+            squashed = {}
+            for b in range(BATCH):
+                squashed[b] = cell_tile("squashed")
+                nc.scalar.activation(out=squashed[b][:], in_=new_cell[(h_tile, b)][:], func=ACT.Tanh)
+            for b in range(BATCH):
+                new_hidden[(h_tile, b)] = cell_tile("new_hidden")
+                nc.vector.tensor_tensor(
+                    out=new_hidden[(h_tile, b)][:],
+                    in0=squashed[b][:],
+                    in1=activated[(h_tile, 3, b)][:],
+                    op=ALU.mult,
+                )
+                nc.sync.dma_start(out=out_1[b, h_rows, :], in_=new_hidden[(h_tile, b)][:])
 
         def store_hidden_transposed(h_tile):
-            bank = bank_pool.tile([P, BANK_WORDS], F32, name="bank")
-            for r in range(ROW_TILES):
-                tile_columns = slice(r * P, (r + 1) * P)
-                nc.tensor.transpose(
-                    bank[:, tile_columns], new_hidden[h_tile][:, tile_columns], identity[:]
+            h_columns = slice(h_tile * P, (h_tile + 1) * P)
+            for b in range(BATCH):
+                bank = bank_pool.tile([P, BANK_WORDS], F32, name="bank")
+                for t in range(FRAMES // P):
+                    frames = slice(t * P, (t + 1) * P)
+                    nc.tensor.transpose(bank[:, frames], new_hidden[(h_tile, b)][:, frames], identity[:])
+                flipped = cell_tile("flipped")
+                copy_out = nc.scalar.copy if b == 0 else nc.vector.tensor_copy
+                copy_out(out=flipped[:], in_=bank[:, :FRAMES])
+                nc.sync.dma_start(
+                    out=out_0[b].rearrange("(t p) h -> p t h", p=P)[:, :, h_columns],
+                    in_=flipped[:].rearrange("p (t h) -> p t h", h=P),
                 )
-            flipped = cell_pool.tile([P, N], F32, name="flipped")
-            nc.vector.tensor_copy(out=flipped[:], in_=bank[:])
-            nc.sync.dma_start(
-                out=out_0.rearrange("b (t p) h -> p (b t) h", p=P)[:, :, h_tile * P : (h_tile + 1) * P],
-                in_=flipped[:].rearrange("p (r h) -> p r h", r=ROW_TILES),
-            )
 
         def h_tile_closed_by(index):
             if 0 <= index < len(rounds) and rounds[index][1][-1] == PASSES - 1:
@@ -277,19 +305,19 @@ def tile_batchedlstm_k_kernel(
 
         for step in range(LOAD_AHEAD):
             load_chunk(step)
-        for index in range(len(rounds) + 3):
-            if h_tile_closed_by(index - 3) is not None:
-                store_hidden_transposed(h_tile_closed_by(index - 3))
+        for index in range(len(rounds) + FLIP_LAG + 1):
+            if h_tile_closed_by(index - FLIP_LAG) is not None:
+                store_hidden_transposed(h_tile_closed_by(index - FLIP_LAG))
             if index < len(rounds):
                 stage(index)
-            if index == 0:
-                prepare_small_inputs()
             if 0 <= index - 1 < len(rounds):
                 multiply(index - 1)
             if h_tile_closed_by(index - 2) is not None:
                 update_cell(h_tile_closed_by(index - 2))
             if index < len(rounds):
                 quantise(index)
+            if index == 0:
+                prepare_small_inputs()
             if h_tile_closed_by(index - 1) is not None:
                 activate_gates(h_tile_closed_by(index - 1))
             if h_tile_closed_by(index - 2) is not None:

@@ -35,7 +35,6 @@ OPERAND_BANKS = 2
 BANK_TILES = 2
 BANK_COLUMNS = BANK_TILES * P
 
-IDLE_MATMULS = 3
 FLIP_LAG = 5
 
 FLOPS = 2 * GATES * HIDDEN * K * N
@@ -68,8 +67,6 @@ def tile_batchedlstm_k_kernel(
 
         identity = keep.tile([P, P], F32, name="identity")
         make_identity(nc, identity[:])
-        zeros = keep.tile([P, N], BF16, name="zeros")
-        nc.vector.memset(zeros[:], 0.0)
 
         bias_rows = keep.tile([P, P], BF16, name="bias_rows")
         nc.vector.memset(bias_rows[:], 0.0)
@@ -100,12 +97,6 @@ def tile_batchedlstm_k_kernel(
                 out=last_xh[:].rearrange("p (b f t) -> p b f t", b=BATCH, t=PACK)[:, :, :, 2:4],
                 in_=hidden_raw[:].rearrange("p b (e f) -> p b f e", e=2),
             )
-
-        idle_bank = acc_pool.tile([P, N], F32, name="acc0")
-
-        def hold_clock():
-            for repeat in range(IDLE_MATMULS):
-                nc.tensor.matmul(idle_bank[:], lhsT=zeros[:, :P], rhs=zeros[:], start=True, stop=True)
 
         x_raw = {}
         w_raw = {}
@@ -184,8 +175,6 @@ def tile_batchedlstm_k_kernel(
                         transpose_operand(index, sources, first_word, x_codes[g], x_scales[g], True)
                     else:
                         transpose_last_xh(index, sources, first_word, x_codes[g], x_scales[g])
-                    if index == 0:
-                        hold_clock()
                 step = h_tile * CHUNKS + chunk
                 if pass_in_chunk == 0 and step + LOAD_AHEAD < H_TILES * CHUNKS:
                     load_chunk(step + LOAD_AHEAD)
@@ -196,8 +185,6 @@ def tile_batchedlstm_k_kernel(
                 w_scales[(h_tile, g)] = scales
                 first_operand = len(staged[index]) == 0
                 transpose_operand(index, sources, first_word, codes, scales, first_operand)
-                if index == 0:
-                    hold_clock()
 
         def quantise(index):
             for grouped, codes, scales in staged[index]:

from contextlib import ExitStack

import concourse.mybir as mybir
from concourse.masks import make_identity

F32 = mybir.dt.float32
BF16 = mybir.dt.bfloat16
U32 = mybir.dt.uint32
U8 = mybir.dt.uint8
FP8X4 = mybir.dt.float8_e4m3fn_x4
ACT = mybir.ActivationFunctionType
ALU = mybir.AluOpType

P = 128
PACK = 4
K_PASS = P * PACK
PASS_WORDS = K_PASS // 2
BANK_WORDS = 512

BATCH, FRAMES, CHANNELS, HIDDEN = 2, 256, 7936, 256
K = CHANNELS + HIDDEN
PASSES = K // K_PASS
N = BATCH * FRAMES
ROW_TILES = N // P
GATES = 4
H_TILES = HIDDEN // P

CHUNK_PASSES = 2
CHUNK_K = CHUNK_PASSES * K_PASS
CHUNKS = K // CHUNK_K
LOAD_AHEAD = 3

FREE_BANKS = 4
OPERAND_BANKS = 2
BANK_TILES = 2
BANK_COLUMNS = BANK_TILES * P

FLIP_LAG = 5

FLOPS = 2 * GATES * HIDDEN * K * N


def tile_batchedlstm_k_kernel(
    tc, x, hidden_state, cell_state, W_f, b_f, W_i, b_i, W_o, b_o, W_g, b_g, out_0, out_1, out_2
):
    nc = tc.nc
    weights = (W_f, W_i, W_g, W_o)
    biases = (b_f, b_i, b_g, b_o)
    gate_functions = (ACT.Sigmoid, ACT.Sigmoid, ACT.Tanh, ACT.Sigmoid)
    x_rows = x.rearrange("b f c -> (b f) c")

    rounds = []
    for h_tile, operands_a_pass in ((0, 2), (1, 1)):
        round_passes = FREE_BANKS // (OPERAND_BANKS * operands_a_pass)
        rounds += [(h_tile, list(range(g, g + round_passes))) for g in range(0, PASSES, round_passes)]

    with ExitStack() as ctx:
        ctx.enter_context(tc.manual_schedule())
        keep = ctx.enter_context(tc.tile_pool(name="keep", bufs=1))
        x_raw_pool = ctx.enter_context(tc.tile_pool(name="x_raw", bufs=ROW_TILES * (LOAD_AHEAD + 1)))
        w_raw_pool = ctx.enter_context(tc.tile_pool(name="w_raw", bufs=GATES * (LOAD_AHEAD + 1)))
        grouped_pool = ctx.enter_context(tc.tile_pool(name="grouped", bufs=2 * FREE_BANKS))
        w_mx_pool = ctx.enter_context(tc.tile_pool(name="w_mx", bufs=4))
        cell_pool = ctx.enter_context(tc.tile_pool(name="cell", bufs=H_TILES * BATCH))
        acc_pool = ctx.enter_context(tc.psum_pool(name="acc", bufs=1))
        bank_pool = ctx.enter_context(tc.psum_pool(name="bank", bufs=FREE_BANKS))

        identity = keep.tile([P, P], F32, name="identity")
        make_identity(nc, identity[:])

        bias_rows = keep.tile([P, P], BF16, name="bias_rows")
        nc.vector.memset(bias_rows[:], 0.0)
        for gate in range(GATES):
            nc.scalar.dma_start(
                out=bias_rows[gate * H_TILES : (gate + 1) * H_TILES, :],
                in_=biases[gate].rearrange("(t p) -> t p", p=P),
            )
        bias_columns = keep.tile([P, GATES * H_TILES], F32, name="bias_columns")

        hidden_raw = keep.tile([P, BATCH, 2 * FRAMES], BF16, name="hidden_raw")
        nc.scalar.dma_start(
            out=hidden_raw[:], in_=hidden_state.rearrange("b (p e) f -> p b (e f)", e=2)
        )
        last_xh = keep.tile([P, N * PACK], BF16, align_bytes=64, name="last_xh")

        warm = keep.tile([P, 1], F32, name="warm")
        nc.vector.memset(warm[:], 0.0)
        nc.scalar.activation(out=warm[:], in_=warm[:], func=ACT.Sigmoid)

        def prepare_small_inputs():
            bias_rows_f32 = keep.tile([P, P], F32, name="bias_rows_f32")
            nc.vector.tensor_copy(out=bias_rows_f32[:], in_=bias_rows[:])
            bank = bank_pool.tile([P, BANK_WORDS], F32, name="bank")
            nc.tensor.transpose(bank[:, :P], bias_rows_f32[:], identity[:])
            nc.vector.tensor_copy(out=bias_columns[:], in_=bank[:, : GATES * H_TILES])
            nc.vector.tensor_copy(
                out=last_xh[:].rearrange("p (b f t) -> p b f t", b=BATCH, t=PACK)[:, :, :, 2:4],
                in_=hidden_raw[:].rearrange("p b (e f) -> p b f e", e=2),
            )

        x_raw = {}
        w_raw = {}
        cell_raw = {}

        def load_chunk(step):
            h_tile, chunk = divmod(step, CHUNKS)
            h_rows = slice(h_tile * P, (h_tile + 1) * P)
            k0 = chunk * CHUNK_K
            if h_tile == 0:
                width = min(CHUNK_K, CHANNELS - k0)
                for r in range(ROW_TILES):
                    raw = x_raw_pool.tile([P, CHUNK_K], BF16, name="x_raw")
                    nc.sync.dma_start(
                        out=raw[:, :width], in_=x_rows[r * P : (r + 1) * P, k0 : k0 + width]
                    )
                    x_raw[(chunk, r)] = raw
            for gate in range(GATES):
                raw = w_raw_pool.tile([P, CHUNK_K], BF16, name="w_raw")
                nc.sync.dma_start(out=raw[:], in_=weights[gate][h_rows, k0 : k0 + CHUNK_K])
                w_raw[(h_tile, chunk, gate)] = raw
            if chunk == CHUNKS - 1:
                raw = cell_pool.tile([P, BATCH, FRAMES], BF16, name="cell_raw")
                nc.sync.dma_start(out=raw[:], in_=cell_state.rearrange("b h f -> h b f")[h_rows])
                cell_raw[h_tile] = raw

        staged = {}

        def transpose_operand(index, sources, first_word, codes, scales, vector_helps):
            for half in range(OPERAND_BANKS):
                bank = bank_pool.tile([P, BANK_WORDS], F32, name="bank")
                planes = bank[:].rearrange("p (s u n) -> p s u n", s=BANK_TILES, u=2)
                for s in range(BANK_TILES):
                    words = sources[BANK_TILES * half + s][:].bitcast(F32)
                    for u in range(2):
                        w0 = first_word + u * P
                        nc.tensor.transpose(planes[:, s, u, :], words[:, w0 : w0 + P], identity[:])
                grouped = grouped_pool.tile(
                    [P, BANK_COLUMNS * PACK], BF16, align_bytes=64, name="grouped"
                )
                copy_out = nc.vector.tensor_copy if vector_helps and half == 1 else nc.scalar.copy
                copy_out(
                    out=grouped[:].bitcast(F32).rearrange("p (s n u) -> p s n u", s=BANK_TILES, u=2),
                    in_=planes.rearrange("p s u n -> p s n u"),
                )
                columns = slice(half * BANK_COLUMNS, (half + 1) * BANK_COLUMNS)
                staged[index].append((grouped[:], codes[:, columns], scales[:, columns]))

        def transpose_last_xh(index, sources, first_word, codes, scales):
            bank = bank_pool.tile([P, BANK_WORDS], F32, name="bank")
            for r in range(ROW_TILES):
                words = sources[r][:].bitcast(F32)
                nc.tensor.transpose(
                    bank[:, r * P : (r + 1) * P], words[:, first_word : first_word + P], identity[:]
                )
            last_xh_words = last_xh[:].bitcast(F32).rearrange("p (n u) -> p n u", u=2)
            nc.vector.tensor_copy(out=last_xh_words[:, :, 0], in_=bank[:])
            staged[index].append((last_xh[:], codes[:], scales[:]))

        x_codes = {}
        x_scales = {}
        w_codes = {}
        w_scales = {}

        def stage(index):
            h_tile, passes = rounds[index]
            staged[index] = []
            for g in passes:
                chunk, pass_in_chunk = divmod(g, CHUNK_PASSES)
                first_word = pass_in_chunk * PASS_WORDS
                if h_tile == 0:
                    sources = [x_raw[(chunk, r)] for r in range(ROW_TILES)]
                    x_codes[g] = keep.tile([P, N], U32, align_bytes=64, name="x_codes%d" % g)
                    x_scales[g] = keep.tile([P, N], U8, align_bytes=64, name="x_scales%d" % g)
                    if g < PASSES - 1:
                        transpose_operand(index, sources, first_word, x_codes[g], x_scales[g], True)
                    else:
                        transpose_last_xh(index, sources, first_word, x_codes[g], x_scales[g])
                step = h_tile * CHUNKS + chunk
                if pass_in_chunk == 0 and step + LOAD_AHEAD < H_TILES * CHUNKS:
                    load_chunk(step + LOAD_AHEAD)
                sources = [w_raw[(h_tile, chunk, gate)] for gate in range(GATES)]
                codes = w_mx_pool.tile([P, GATES * P], U32, align_bytes=64, name="w_codes")
                scales = w_mx_pool.tile([P, GATES * P], U8, align_bytes=64, name="w_scales")
                w_codes[(h_tile, g)] = codes
                w_scales[(h_tile, g)] = scales
                first_operand = len(staged[index]) == 0
                transpose_operand(index, sources, first_word, codes, scales, first_operand)

        def quantise(index):
            for grouped, codes, scales in staged[index]:
                nc.vector.quantize_mx(out=codes.bitcast(FP8X4), scales=scales, in_=grouped)

        acc = {}

        def multiply(index):
            h_tile, passes = rounds[index]
            for gate in range(GATES):
                if passes[0] == 0:
                    acc[(h_tile, gate)] = acc_pool.tile([P, N], F32, name="acc%d" % gate)
                gate_columns = slice(gate * P, (gate + 1) * P)
                for g in passes:
                    nc.tensor.matmul_mx(
                        out=acc[(h_tile, gate)][:],
                        lhsT=w_codes[(h_tile, g)][:, gate_columns].bitcast(FP8X4),
                        lhsT_scale=w_scales[(h_tile, g)][:, gate_columns],
                        rhs=x_codes[g][:].bitcast(FP8X4),
                        rhs_scale=x_scales[g][:],
                        start=(g == 0),
                        stop=(g == PASSES - 1),
                    )

        activated = {}
        new_cell = {}
        new_hidden = {}

        def cell_tile(name):
            return cell_pool.tile([P, FRAMES], F32, name=name)

        def activate_gates(h_tile):
            for gate in range(GATES):
                bias_column = gate * H_TILES + h_tile
                for b in range(BATCH):
                    activated[(h_tile, gate, b)] = cell_tile("gate%d" % gate)
                    nc.scalar.activation(
                        out=activated[(h_tile, gate, b)][:],
                        in_=acc[(h_tile, gate)][:, b * FRAMES : (b + 1) * FRAMES],
                        func=gate_functions[gate],
                        bias=bias_columns[:, bias_column : bias_column + 1],
                        scale=1.0,
                    )

        def update_cell(h_tile):
            h_rows = slice(h_tile * P, (h_tile + 1) * P)
            kept = {}
            for b in range(BATCH):
                kept[b] = cell_tile("kept")
                nc.vector.tensor_tensor(
                    out=kept[b][:],
                    in0=activated[(h_tile, 0, b)][:],
                    in1=cell_raw[h_tile][:, b, :],
                    op=ALU.mult,
                )
            for b in range(BATCH):
                added = cell_tile("added")
                nc.vector.tensor_tensor(
                    out=added[:],
                    in0=activated[(h_tile, 1, b)][:],
                    in1=activated[(h_tile, 2, b)][:],
                    op=ALU.mult,
                )
                new_cell[(h_tile, b)] = cell_tile("new_cell")
                nc.vector.tensor_tensor(
                    out=new_cell[(h_tile, b)][:], in0=kept[b][:], in1=added[:], op=ALU.add
                )
                nc.sync.dma_start(out=out_2[b, h_rows, :], in_=new_cell[(h_tile, b)][:])

        def update_hidden(h_tile):
            h_rows = slice(h_tile * P, (h_tile + 1) * P)
            squashed = {}
            for b in range(BATCH):
                squashed[b] = cell_tile("squashed")
                nc.scalar.activation(out=squashed[b][:], in_=new_cell[(h_tile, b)][:], func=ACT.Tanh)
            for b in range(BATCH):
                new_hidden[(h_tile, b)] = cell_tile("new_hidden")
                nc.vector.tensor_tensor(
                    out=new_hidden[(h_tile, b)][:],
                    in0=squashed[b][:],
                    in1=activated[(h_tile, 3, b)][:],
                    op=ALU.mult,
                )
                nc.sync.dma_start(out=out_1[b, h_rows, :], in_=new_hidden[(h_tile, b)][:])

        def store_hidden_transposed(h_tile):
            h_columns = slice(h_tile * P, (h_tile + 1) * P)
            for b in range(BATCH):
                bank = bank_pool.tile([P, BANK_WORDS], F32, name="bank")
                for t in range(FRAMES // P):
                    frames = slice(t * P, (t + 1) * P)
                    nc.tensor.transpose(bank[:, frames], new_hidden[(h_tile, b)][:, frames], identity[:])
                flipped = cell_tile("flipped")
                copy_out = nc.scalar.copy if b == 0 else nc.vector.tensor_copy
                copy_out(out=flipped[:], in_=bank[:, :FRAMES])
                nc.sync.dma_start(
                    out=out_0[b].rearrange("(t p) h -> p t h", p=P)[:, :, h_columns],
                    in_=flipped[:].rearrange("p (t h) -> p t h", h=P),
                )

        def h_tile_closed_by(index):
            if 0 <= index < len(rounds) and rounds[index][1][-1] == PASSES - 1:
                return rounds[index][0]
            return None

        for step in range(LOAD_AHEAD):
            load_chunk(step)
        for index in range(len(rounds) + FLIP_LAG + 1):
            if h_tile_closed_by(index - FLIP_LAG) is not None:
                store_hidden_transposed(h_tile_closed_by(index - FLIP_LAG))
            if index < len(rounds):
                stage(index)
            if 0 <= index - 1 < len(rounds):
                multiply(index - 1)
            if h_tile_closed_by(index - 2) is not None:
                update_cell(h_tile_closed_by(index - 2))
            if index < len(rounds):
                quantise(index)
            if index == 0:
                prepare_small_inputs()
            if h_tile_closed_by(index - 1) is not None:
                activate_gates(h_tile_closed_by(index - 1))
            if h_tile_closed_by(index - 2) is not None:
                update_hidden(h_tile_closed_by(index - 2))
